import numpy as np
import ml_dtypes


def mxq(x, axis, fmt="e4m3"):
    dtype, down = {"e4m3": (ml_dtypes.float8_e4m3fn, 7), "e5m2": (ml_dtypes.float8_e5m2, 14)}[fmt]
    v = np.moveaxis(np.asarray(x, np.float32).astype(ml_dtypes.bfloat16).astype(np.float64), axis, -1)
    blocks = v.reshape(v.shape[:-1] + (-1, 32))
    amax = np.abs(blocks).max(-1, keepdims=True)
    byte = np.maximum(np.where(amax > 0, np.frexp(amax)[1] - 1 + 127, 0) - down, 1)
    scale = np.exp2(byte - 127.0)
    codes = (blocks / scale).astype(np.float32).astype(dtype).astype(np.float64)
    return np.moveaxis((codes * scale).reshape(v.shape), -1, axis)


WIDE = False


def mx_kscale(k):
    if not WIDE:
        return np.ones(k)
    levels = np.array([10, -10, 5, -5, 0])
    if k % 512:
        return np.exp2(np.random.permutation(np.resize(levels, k // 32))).repeat(32)
    a = np.empty((k // 512, 16))
    for p in range(k // 512):
        a[p, :8] = np.random.permutation(np.resize(levels, 8))
        for g in range(8):
            far = levels[np.abs(levels - a[p, g]) >= 10]
            a[p, g + 8] = far[np.random.randint(len(far))]
    return np.exp2(a.ravel()).repeat(32)


BF16 = ml_dtypes.bfloat16


def bf(x):
    return np.asarray(x, np.float32).astype(BF16)


def f64(x):
    return np.asarray(x).astype(np.float64)


B, S, D_IN, D_OUT = 3, 512, 1024, 1024


def relative_shift(x):
    b, s, d = x.shape
    padded = np.concatenate([np.zeros((b, 1, d)), x], axis=1).reshape(s + 1, b, d)
    return padded[1:].reshape(b, s, d)


def setup_inputs():
    s = mx_kscale(D_IN)
    return {"pos_embed": bf(np.random.standard_normal((B, S, D_IN)) * s),
            "W_r": bf(np.random.standard_normal((D_OUT, D_IN)) * 1.2 / np.sqrt(D_IN) / s[None, :]),
            "b_r": bf(np.random.standard_normal(D_OUT) * 0.3)}


def reference(pos_embed, W_r, b_r):
    shifted = relative_shift(f64(pos_embed))
    return (mxq(shifted, 2, "e4m3") @ mxq(f64(W_r), 1, "e4m3").T) + f64(b_r)

from contextlib import ExitStack

import concourse.mybir as mybir
from concourse.masks import make_identity

F32 = mybir.dt.float32
BF16 = mybir.dt.bfloat16
U32 = mybir.dt.uint32
U8 = mybir.dt.uint8
FP8X4 = mybir.dt.float8_e4m3fn_x4

P = 128
D_IN = 1024
D_OUT = 1024
ROWS = 3 * 512
PASSES = D_IN // 512
WORDS = D_IN // 2
SECTIONS = 3
LANES = 4
FIRST_LANES = (0, 1)
LAST_LANES = (2, 3)
HALVES = 2
N_HALF = D_OUT // HALVES
W_TILES = N_HALF // P

FLOPS = 2 * ROWS * D_IN * D_OUT


def tile_relativemultiheadattention_pa_kernel(tc, pos_embed, W_r, b_r, out):
    nc = tc.nc
    x_rows = pos_embed.flatten_outer_dims()
    out_rows = out.flatten_outer_dims()

    with ExitStack() as stack:
        keep = stack.enter_context(tc.tile_pool(name="keep", bufs=1))
        turned_pool = stack.enter_context(tc.psum_pool(name="turned_pool", bufs=4))
        sums_pool = stack.enter_context(tc.psum_pool(name="sums_pool", bufs=4))
        stack.enter_context(tc.manual_schedule())

        x_raw = [keep.tile([P, LANES * D_IN], BF16, name="x_raw%d" % s) for s in range(SECTIONS)]
        w_raw = [keep.tile([P, W_TILES * D_IN], BF16, name="w_raw%d" % h) for h in range(HALVES)]
        x_grouped = [
            keep.tile([P, LANES * PASSES * P * 4], BF16, name="x_grouped%d" % s, align_bytes=64)
            for s in range(SECTIONS)
        ]
        w_grouped = [
            keep.tile([P, PASSES * N_HALF * 4], BF16, name="w_grouped%d" % h, align_bytes=64)
            for h in range(HALVES)
        ]
        x_codes = [
            keep.tile([P, LANES * PASSES * P], U32, name="x_codes%d" % s, align_bytes=64)
            for s in range(SECTIONS)
        ]
        x_scales = [
            keep.tile([P, LANES * PASSES * P], U8, name="x_scales%d" % s, align_bytes=64)
            for s in range(SECTIONS)
        ]
        w_codes = [
            keep.tile([P, PASSES * N_HALF], U32, name="w_codes%d" % h, align_bytes=64)
            for h in range(HALVES)
        ]
        w_scales = [
            keep.tile([P, PASSES * N_HALF], U8, name="w_scales%d" % h, align_bytes=64)
            for h in range(HALVES)
        ]
        result = [keep.tile([P, LANES * D_OUT], F32, name="result%d" % s) for s in range(SECTIONS)]
        identity = keep.tile([P, P], F32, name="identity")
        ones = keep.tile([P, P], BF16, name="ones")
        bias_row = keep.tile([P, D_OUT], BF16, name="bias_row")
        bias_all = keep.tile([P, D_OUT], F32, name="bias_all")

        def load_w_half(h):
            for j in range(W_TILES):
                first = N_HALF * h + P * j
                nc.sync.dma_start(
                    out=w_raw[h][:, D_IN * j : D_IN * (j + 1)], in_=W_r[first : first + P, :]
                )

        def load_x_section(s):
            first = 512 * s + 2 - s
            rows = x_rows[first : first + 512, :].rearrange("(p t) k -> p (t k)", t=LANES)
            for cols in (slice(0, 2 * D_IN), slice(2 * D_IN, 4 * D_IN)):
                nc.sync.dma_start(out=x_raw[s][:, cols], in_=rows[:, cols])

        nc.vector.memset(bias_row[:], 0.0)
        nc.scalar.dma_start(out=bias_row[0:1, :], in_=b_r.rearrange("(o n) -> o n", o=1))
        load_w_half(0)
        load_x_section(0)
        load_w_half(1)
        load_x_section(1)
        load_x_section(2)

        make_identity(nc, identity[:])
        nc.vector.memset(ones[:], 1.0)

        def turn(raw, tile_index, grouped_words):
            words = raw[:].bitcast(F32)
            turned = turned_pool.tile([P, WORDS], F32, tag="turned")
            for w in range(WORDS // P):
                g, u = divmod(w, 2)
                first = WORDS * tile_index + 2 * P * g
                nc.tensor.transpose(
                    out=turned[:, P * w : P * (w + 1)],
                    in_=words[:, first + u : first + 2 * P : 2],
                    identity=identity[:],
                )
            nc.scalar.copy(
                out=grouped_words,
                in_=turned[:].rearrange("p (g u r) -> p g r u", g=PASSES, u=2),
            )

        def prepare_w_half(h):
            words = w_grouped[h][:].bitcast(F32).rearrange("p (g n u) -> p g n u", g=PASSES, u=2)
            for j in range(W_TILES):
                turn(w_raw[h], j, words[:, :, P * j : P * (j + 1), :])
            for g in range(PASSES):
                feats = slice(N_HALF * g, N_HALF * (g + 1))
                nc.vector.quantize_mx(
                    out=w_codes[h][:, feats].bitcast(FP8X4),
                    scales=w_scales[h][:, feats],
                    in_=w_grouped[h][:, 4 * N_HALF * g : 4 * N_HALF * (g + 1)],
                )

        def mend_shift(s, words):
            if s == 0:
                nc.vector.tensor_copy(out=words[:, 3, :, P - 1, :], in_=words[:, 2, :, P - 1, :])
                nc.vector.memset(words[:, 2, :, P - 1, :], 0.0)
            if s == 1:
                nc.vector.memset(words[:, 3, :, P - 1, :], 0.0)

        def x_words(s):
            return x_grouped[s][:].bitcast(F32).rearrange(
                "p (l g r u) -> p l g r u", l=LANES, g=PASSES, u=2
            )

        def turn_x_section(s):
            for lane in range(LANES):
                turn(x_raw[s], lane, x_words(s)[:, lane, :, :, :])

        def quantise_x_lanes(s, lanes):
            if lanes == LAST_LANES:
                mend_shift(s, x_words(s))
            first = PASSES * P * lanes[0]
            width = PASSES * P * len(lanes)
            nc.vector.quantize_mx(
                out=x_codes[s][:, first : first + width].bitcast(FP8X4),
                scales=x_scales[s][:, first : first + width],
                in_=x_grouped[s][:, 4 * first : 4 * (first + width)],
            )

        def multiply(s, lane, h):
            sums = sums_pool.tile([P, N_HALF], F32, tag="sums")
            for g in range(PASSES):
                rows = slice(P * (PASSES * lane + g), P * (PASSES * lane + g + 1))
                feats = slice(N_HALF * g, N_HALF * (g + 1))
                nc.tensor.matmul_mx(
                    out=sums[:],
                    lhsT=x_codes[s][:, rows].bitcast(FP8X4),
                    lhsT_scale=x_scales[s][:, rows],
                    rhs=w_codes[h][:, feats].bitcast(FP8X4),
                    rhs_scale=w_scales[h][:, feats],
                    start=(g == 0),
                    stop=(g == PASSES - 1),
                )
            first = D_OUT * lane + N_HALF * h
            nc.vector.tensor_tensor(
                out=result[s][:, first : first + N_HALF],
                in0=sums[:],
                in1=bias_all[:, N_HALF * h : N_HALF * (h + 1)],
                op=mybir.AluOpType.add,
            )

        def spread_bias():
            for h in range(HALVES):
                cols = slice(N_HALF * h, N_HALF * (h + 1))
                spread = sums_pool.tile([P, N_HALF], F32, tag="sums")
                nc.tensor.matmul(
                    out=spread[:], lhsT=ones[:], rhs=bias_row[:, cols], start=True, stop=True
                )
                nc.vector.tensor_copy(out=bias_all[:, cols], in_=spread[:])

        def store(s, lane, first, width):
            rows = out_rows[512 * s : 512 * (s + 1), :].rearrange("(p t) d -> p (t d)", t=LANES)
            cols = slice(D_OUT * lane + first, D_OUT * lane + first + width)
            nc.sync.dma_start(out=rows[:, cols], in_=result[s][:, cols])

        def multiply_half(s, lanes, h):
            for lane in lanes:
                multiply(s, lane, h)
                store(s, lane, N_HALF * h, N_HALF)

        def multiply_whole(s, lanes):
            for lane in lanes:
                for h in range(HALVES):
                    multiply(s, lane, h)
                store(s, lane, 0, D_OUT)

        prepare_w_half(0)
        spread_bias()
        turn_x_section(0)
        quantise_x_lanes(0, FIRST_LANES)
        quantise_x_lanes(0, LAST_LANES)
        prepare_w_half(1)
        multiply_half(0, FIRST_LANES, 0)
        multiply_half(0, LAST_LANES, 0)
        turn_x_section(1)
        multiply_half(0, FIRST_LANES, 1)
        quantise_x_lanes(1, FIRST_LANES)
        multiply_half(0, LAST_LANES, 1)
        quantise_x_lanes(1, LAST_LANES)
        turn_x_section(2)
        multiply_whole(1, FIRST_LANES[:1])
        quantise_x_lanes(2, FIRST_LANES)
        multiply_whole(1, FIRST_LANES[1:])
        quantise_x_lanes(2, LAST_LANES)
        multiply_whole(1, LAST_LANES)
        multiply_whole(2, FIRST_LANES)
        multiply_whole(2, LAST_LANES[:1])
        multiply_half(2, LAST_LANES[1:], 0)
        multiply_half(2, LAST_LANES[1:], 1)
